import numpy as np
import ml_dtypes


def mxq(x, axis, fmt="e4m3"):
    dtype, down = {"e4m3": (ml_dtypes.float8_e4m3fn, 7), "e5m2": (ml_dtypes.float8_e5m2, 14)}[fmt]
    v = np.moveaxis(np.asarray(x, np.float32).astype(ml_dtypes.bfloat16).astype(np.float64), axis, -1)
    blocks = v.reshape(v.shape[:-1] + (-1, 32))
    amax = np.abs(blocks).max(-1, keepdims=True)
    byte = np.maximum(np.where(amax > 0, np.frexp(amax)[1] - 1 + 127, 0) - down, 1)
    scale = np.exp2(byte - 127.0)
    codes = (blocks / scale).astype(np.float32).astype(dtype).astype(np.float64)
    return np.moveaxis((codes * scale).reshape(v.shape), -1, axis)


WIDE = False


def mx_kscale(k):
    if not WIDE:
        return np.ones(k)
    levels = np.array([10, -10, 5, -5, 0])
    if k % 512:
        return np.exp2(np.random.permutation(np.resize(levels, k // 32))).repeat(32)
    a = np.empty((k // 512, 16))
    for p in range(k // 512):
        a[p, :8] = np.random.permutation(np.resize(levels, 8))
        for g in range(8):
            far = levels[np.abs(levels - a[p, g]) >= 10]
            a[p, g + 8] = far[np.random.randint(len(far))]
    return np.exp2(a.ravel()).repeat(32)


BF16 = ml_dtypes.bfloat16


def bf(x):
    return np.asarray(x, np.float32).astype(BF16)


def f64(x):
    return np.asarray(x).astype(np.float64)


B, C, W, H = 8, 512, 16, 32


def setup_inputs():
    t = mx_kscale(C)
    return {"x1": bf(np.random.standard_normal((B, W, H, C)) * t),
            "x2": bf(np.random.standard_normal((B, W, H, C)) * t),
            "x3": bf(np.random.standard_normal((B, W, H, C)) * t),
            "hat": bf(np.random.standard_normal((B, 3 * C))),
            "w2": bf(np.random.standard_normal((C, C)) / np.sqrt(C) / t[None, :]),
            "b2": bf(np.random.standard_normal(C) * 0.1)}


def reference(x1, x2, x3, hat, w2, b2):
    hs = f64(hat).reshape(-1, 3, C)
    e = np.exp(hs - hs.max(axis=1, keepdims=True))
    bar = e / e.sum(axis=1, keepdims=True)
    g = bar[:, :, None, None, :]
    out = g[:, 0] * f64(x1) + g[:, 1] * f64(x2) + g[:, 2] * f64(x3)
    z = (mxq(out, 3, "e4m3") @ mxq(f64(w2), 1, "e4m3").T) + f64(b2)
    return z.transpose(0, 3, 1, 2)

@@ -1,0 +1,269 @@
+from contextlib import ExitStack
+
+import concourse.mybir as mybir
+from concourse.masks import make_identity
+
+F32 = mybir.dt.float32
+BF16 = mybir.dt.bfloat16
+U32 = mybir.dt.uint32
+U8 = mybir.dt.uint8
+FP8X4 = mybir.dt.float8_e4m3fn_x4
+ALU = mybir.AluOpType
+ACT = mybir.ActivationFunctionType
+AX = mybir.AxisListType
+
+P = 128
+B = 8
+C = 512
+TOK = 512
+UNITS = 2 * B
+FLOPS = 2 * B * TOK * C * C
+
+
+def tile_modelnew_pb_t_kernel(tc, x1, x2, x3, hat, w2, b2, out):
+    nc = tc.nc
+    xs = [x1, x2, x3]
+    with ExitStack() as ctx:
+        const = ctx.enter_context(tc.tile_pool(name="const", bufs=1))
+        xin = ctx.enter_context(tc.tile_pool(name="xin", bufs=B))
+        work = ctx.enter_context(tc.tile_pool(name="work", bufs=4))
+        stage = ctx.enter_context(tc.tile_pool(name="stage", bufs=4))
+        psum = ctx.enter_context(tc.psum_pool(name="psum", bufs=2))
+        ctx.enter_context(tc.manual_schedule())
+
+        hat_sb = const.tile([P, C], BF16)
+        hat_rows = hat.rearrange("b (k c) -> (b k) c", k=3)
+        nc.sync.dma_start(out=hat_sb[0:16, :], in_=hat_rows[0:16, :])
+        nc.scalar.dma_start(out=hat_sb[16:24, :], in_=hat_rows[16:24, :])
+        nc.scalar.dma_start(out=hat_sb[24:32, :], in_=hat_rows[0:8, :])
+        nc.vector.memset(hat_sb[32:64, :], 0.0)
+        nc.vector.memset(hat_sb[64:128, :], 0.0)
+        b2_bf = const.tile([P, 4], BF16)
+        nc.scalar.dma_start(out=b2_bf[:], in_=b2.rearrange("(i j) -> i j", j=4))
+
+        warm_in = const.tile([P, 1], F32)
+        warm_out = const.tile([P, 1], F32)
+        nc.vector.memset(warm_in[:], 0.0)
+        nc.scalar.activation(out=warm_out[:], in_=warm_in[:], func=ACT.Exp)
+
+        ident = const.tile([P, P], F32)
+        make_identity(nc, ident[:])
+
+        w_sb = const.tile([P, 4, C], BF16)
+        nc.sync.dma_start(out=w_sb[:], in_=w2.rearrange("(i j) c -> i j c", j=4))
+        x_sb = []
+        for b in range(B):
+            row = []
+            for k in range(3):
+                xt = xin.tile([P, 4, C], BF16, name="x%d_%d" % (k, b), tag="x%d" % k)
+                src = xs[k][b].rearrange("w h c -> (w h) c").rearrange("(p j) c -> p j c", j=4)
+                nc.sync.dma_start(out=xt[:], in_=src)
+                row.append(xt)
+            x_sb.append(row)
+
+        aux_ps = psum.tile([P, 2, P], F32, tag="o")
+        hat_w = hat_sb[:].bitcast(F32)
+        for u in range(2):
+            nc.tensor.transpose(aux_ps[:, u, :], hat_w[:, u : 2 * P : 2], ident[:])
+        logit = const.tile([P, 16, 3, 2], F32)
+        nc.vector.tensor_copy(
+            out=logit[:].rearrange("q (u b) k e -> q u (b k e)", u=2),
+            in_=aux_ps[:].bitcast(BF16)[:, :, 0:48],
+        )
+        top = const.tile([P, 16, 2], F32)
+        nc.vector.tensor_reduce(
+            out=top[:], in_=logit[:].rearrange("q a k e -> q a e k"), axis=AX.X, op=ALU.max
+        )
+        shifted = const.tile([P, 16, 3, 2], F32)
+        nc.vector.tensor_tensor(
+            out=shifted[:], in0=logit[:], in1=top[:].unsqueeze(2).to_broadcast([P, 16, 3, 2]),
+            op=ALU.subtract,
+        )
+        expd = const.tile([P, 16, 3, 2], F32)
+        nc.scalar.activation(out=expd[:], in_=shifted[:], func=ACT.Exp)
+        total = const.tile([P, 16, 2], F32)
+        nc.vector.tensor_reduce(
+            out=total[:], in_=expd[:].rearrange("q a k e -> q a e k"), axis=AX.X, op=ALU.add
+        )
+        inv = const.tile([P, 16, 2], F32)
+        nc.vector.reciprocal(out=inv[:], in_=total[:])
+        gate = const.tile([P, 16, 3, 2], F32)
+        nc.vector.tensor_tensor(
+            out=gate[:], in0=expd[:], in1=inv[:].unsqueeze(2).to_broadcast([P, 16, 3, 2]),
+            op=ALU.mult,
+        )
+
+        w_codes = const.tile([P, C], U32, align_bytes=64)
+        w_scales = const.tile([P, C], U8, align_bytes=64)
+        w_grouped = const.tile([P, 4 * C], BF16, align_bytes=64)
+        w_words = w_sb[:].bitcast(F32)
+        w_pairs = w_grouped[:].bitcast(F32).rearrange("q (c u) -> q c u", u=2)
+        for h in range(2):
+            w_ps = psum.tile([P, 2, 2, P], F32, tag="o")
+            for u in range(2):
+                for jj in range(2):
+                    nc.tensor.transpose(
+                        w_ps[:, u, jj, :], w_words[:, 2 * h + jj, u : 2 * P : 2], ident[:]
+                    )
+            copy = nc.vector.tensor_copy if h == 0 else nc.scalar.copy
+            copy(
+                out=w_pairs[:, 256 * h : 256 * h + 256, :],
+                in_=w_ps[:].rearrange("q u jj i -> q (jj i) u"),
+            )
+        b2_f = const.tile([P, 4], F32)
+        nc.vector.tensor_copy(out=b2_f[:], in_=b2_bf[:])
+        nc.vector.quantize_mx(out=w_codes[:].bitcast(FP8X4), scales=w_scales[:], in_=w_grouped[:])
+
+        def half_view(bank, e):
+            v = bank[:].bitcast(BF16).rearrange("q j (p e) -> q j p e", e=2)
+            return v[:, :, :, e].rearrange("q j p -> q p j")
+
+        banks = {}
+        t0s = {}
+        t1s = {}
+        planes = {}
+        grouped = {}
+        codes = {}
+        scales = {}
+        o_sbs = {}
+
+        def gate_of(n, k, e):
+            return gate[:, 8 * (n % 2) + n // 2, k, e : e + 1]
+
+        def transposes(n, k):
+            if n >= UNITS:
+                return
+            b, u = n // 2, n % 2
+            bank = psum.tile([P, 4, P], F32, name="bank%d" % k, tag="t%d" % k)
+            xw = x_sb[b][k][:].bitcast(F32)
+            for j in range(4):
+                nc.tensor.transpose(bank[:, j, :], xw[:, j, u : 2 * P : 2], ident[:])
+            banks[(n, k)] = bank
+
+        def pass1(n):
+            if n >= UNITS:
+                return
+            for e in range(2):
+                t0 = work.tile([P, P, 4], F32, name="t0", bufs=8)
+                nc.scalar.activation(
+                    out=t0[:], in_=half_view(banks[(n, 0)], e), func=ACT.Copy, scale=gate_of(n, 0, e)
+                )
+                t0s[(n, e)] = t0
+
+        def pass2(n, e):
+            t1 = work.tile([P, P, 4], F32, name="t1")
+            nc.vector.scalar_tensor_tensor(
+                out=t1[:], in0=half_view(banks[(n, 1)], e), scalar=gate_of(n, 1, e),
+                in1=t0s[(n, e)][:], op0=ALU.mult, op1=ALU.add,
+            )
+            t1s[(n, e)] = t1
+
+        def pass3(n):
+            b, u = n // 2, n % 2
+            if u == 0:
+                planes[b] = stage.tile([P, 4, TOK], BF16, name="planes")
+            for e in range(2):
+                nc.vector.scalar_tensor_tensor(
+                    out=planes[b][:, 2 * u + e, :].rearrange("q (p j) -> q p j", j=4),
+                    in0=half_view(banks[(n, 2)], e), scalar=gate_of(n, 2, e),
+                    in1=t1s[(n, e)][:], op0=ALU.mult, op1=ALU.add,
+                )
+
+        def regroup(b):
+            grouped[b] = stage.tile([P, TOK, 4], BF16, name="grouped", align_bytes=64)
+            nc.gpsimd.tensor_scalar(
+                out=grouped[b][:], in0=planes[b][:].rearrange("q t n -> q n t"), scalar1=1.0,
+                scalar2=0.0, op0=ALU.mult, op1=ALU.add,
+            )
+
+        def quantise(b, lo, hi):
+            if lo == 0:
+                codes[b] = stage.tile([P, TOK], U32, name="codes", align_bytes=64)
+                scales[b] = stage.tile([P, TOK], U8, name="scales", align_bytes=64)
+            nc.vector.quantize_mx(
+                out=codes[b][:, lo:hi].bitcast(FP8X4), scales=scales[b][:, lo:hi],
+                in_=grouped[b][:, lo:hi, :].rearrange("q n t -> q (n t)"),
+            )
+
+        def one_pass(b, j, lo, hi, tag):
+            acc = psum.tile([P, hi - lo], F32, name="acc", tag=tag)
+            nc.tensor.matmul_mx(
+                out=acc[:],
+                lhsT=w_codes[:, P * j : P * j + P].bitcast(FP8X4),
+                lhsT_scale=w_scales[:, P * j : P * j + P],
+                rhs=codes[b][:, lo:hi].bitcast(FP8X4),
+                rhs_scale=scales[b][:, lo:hi],
+                start=True,
+                stop=True,
+            )
+            return acc
+
+        def way_out(b, j, lo, hi, acc, on_vector):
+            if on_vector:
+                nc.vector.tensor_scalar_add(
+                    out=o_sbs[b][:, j, lo:hi], in0=acc[:], scalar1=b2_f[:, j : j + 1]
+                )
+            else:
+                nc.scalar.activation(
+                    out=o_sbs[b][:, j, lo:hi], in_=acc[:], func=ACT.Identity,
+                    bias=b2_f[:, j : j + 1], scale=1.0,
+                )
+
+        def store(b, j0, lo, hi, eng):
+            dst = out[b].rearrange("(i j) w h -> i j (w h)", j=4)
+            eng.dma_start(out=dst[:, j0 : j0 + 2, lo:hi], in_=o_sbs[b][:, j0 : j0 + 2, lo:hi])
+
+        def project(b, j0, tag):
+            if j0 == 0:
+                o_sbs[b] = stage.tile([P, 4, TOK], F32, name="o_sb")
+            for j in (j0, j0 + 1):
+                way_out(b, j, 0, TOK, one_pass(b, j, 0, TOK, tag), False)
+            store(b, j0, 0, TOK, nc.scalar)
+
+        for n in range(2):
+            for k in range(3):
+                transposes(n, k)
+            pass1(n)
+        transposes(2, 0)
+        pass1(2)
+        for n in range(UNITS):
+            transposes(n + 3, 0)
+            pass1(n + 3)
+            if n % 2 == 0 and n >= 4:
+                project((n - 4) // 2, 2, "o")
+            pass2(n, 0)
+            if n == UNITS - 1:
+                quantise(B - 2, 0, TOK)
+                project(B - 2, 0, "o")
+                project(B - 2, 2, "t0")
+            pass2(n, 1)
+            transposes(n + 2, 1)
+            if n % 2 == 1 and 3 <= n < UNITS - 1:
+                quantise((n - 3) // 2, 0, TOK)
+                project((n - 3) // 2, 0, "o")
+            pass3(n)
+            transposes(n + 2, 2)
+            if n % 2 == 1 and n < UNITS - 1:
+                regroup(n // 2)
+
+        b = B - 1
+        HALF = TOK // 2
+        g = stage.tile([P, TOK, 4], BF16, name="grouped", align_bytes=64)
+        grouped[b] = g
+        src = planes[b][:].rearrange("q t n -> q n t")
+        nc.vector.tensor_copy(out=g[:, 0:HALF, :], in_=src[:, 0:HALF, :])
+        nc.gpsimd.tensor_scalar(
+            out=g[:, 384:TOK, :], in0=src[:, 384:TOK, :], scalar1=1.0, scalar2=0.0,
+            op0=ALU.mult, op1=ALU.add,
+        )
+        nc.vector.tensor_copy(out=g[:, HALF:384, :], in_=src[:, HALF:384, :])
+        quantise(b, 0, HALF)
+        quantise(b, HALF, TOK)
+        o_sbs[b] = stage.tile([P, 4, TOK], F32, name="o_sb")
+        for h, tags in ((0, ("t1", "t1", "t2", "t2")), (1, ("o", "o", "t0", "t0"))):
+            lo, hi = h * HALF, h * HALF + HALF
+            accs = [one_pass(b, j, lo, hi, tags[j]) for j in range(4)]
+            for j in range(4):
+                way_out(b, j, lo, hi, accs[j], j % 2 == 1)
+                if j % 2 == 1:
+                    store(b, j - 1, lo, hi, nc.sync)

@@ -52,7 +52,8 @@ def tile_modelnew_pb_t_kernel(tc, x1, x2, x3, hat, w2, b2, out):
         w_sb = const.tile([P, 4, C], BF16)
         nc.sync.dma_start(out=w_sb[:], in_=w2.rearrange("(i j) c -> i j c", j=4))
         x_sb = []
-        for b in range(B):
+
+        def load(b):
             row = []
             for k in range(3):
                 xt = xin.tile([P, 4, C], BF16, name="x%d_%d" % (k, b), tag="x%d" % k)
@@ -60,6 +61,10 @@ def tile_modelnew_pb_t_kernel(tc, x1, x2, x3, hat, w2, b2, out):
                 nc.sync.dma_start(out=xt[:], in_=src)
                 row.append(xt)
             x_sb.append(row)
+
+        AHEAD = 6
+        for b in range(AHEAD):
+            load(b)
 
         aux_ps = psum.tile([P, 2, P], F32, tag="o")
         hat_w = hat_sb[:].bitcast(F32)
@@ -218,7 +223,9 @@ def tile_modelnew_pb_t_kernel(tc, x1, x2, x3, hat, w2, b2, out):
                 o_sbs[b] = stage.tile([P, 4, TOK], F32, name="o_sb")
             for j in (j0, j0 + 1):
                 way_out(b, j, 0, TOK, one_pass(b, j, 0, TOK, tag), False)
-            store(b, j0, 0, TOK, nc.scalar)
+            store(b, j0, 0, TOK, nc.sync)
+            if j0 == 2 and b + AHEAD < B:
+                load(b + AHEAD)
 
         for n in range(2):
             for k in range(3):

from contextlib import ExitStack

import concourse.mybir as mybir
from concourse.masks import make_identity

F32 = mybir.dt.float32
BF16 = mybir.dt.bfloat16
U32 = mybir.dt.uint32
U8 = mybir.dt.uint8
FP8X4 = mybir.dt.float8_e4m3fn_x4
ALU = mybir.AluOpType
ACT = mybir.ActivationFunctionType
AX = mybir.AxisListType

P = 128
B = 8
C = 512
TOK = 512
UNITS = 2 * B
FLOPS = 2 * B * TOK * C * C


def tile_modelnew_pb_t_kernel(tc, x1, x2, x3, hat, w2, b2, out):
    nc = tc.nc
    xs = [x1, x2, x3]
    with ExitStack() as ctx:
        const = ctx.enter_context(tc.tile_pool(name="const", bufs=1))
        xin = ctx.enter_context(tc.tile_pool(name="xin", bufs=B))
        work = ctx.enter_context(tc.tile_pool(name="work", bufs=4))
        stage = ctx.enter_context(tc.tile_pool(name="stage", bufs=4))
        psum = ctx.enter_context(tc.psum_pool(name="psum", bufs=2))
        ctx.enter_context(tc.manual_schedule())

        hat_sb = const.tile([P, C], BF16)
        hat_rows = hat.rearrange("b (k c) -> (b k) c", k=3)
        nc.sync.dma_start(out=hat_sb[0:16, :], in_=hat_rows[0:16, :])
        nc.scalar.dma_start(out=hat_sb[16:24, :], in_=hat_rows[16:24, :])
        nc.scalar.dma_start(out=hat_sb[24:32, :], in_=hat_rows[0:8, :])
        nc.vector.memset(hat_sb[32:64, :], 0.0)
        nc.vector.memset(hat_sb[64:128, :], 0.0)
        b2_bf = const.tile([P, 4], BF16)
        nc.scalar.dma_start(out=b2_bf[:], in_=b2.rearrange("(i j) -> i j", j=4))

        warm_in = const.tile([P, 1], F32)
        warm_out = const.tile([P, 1], F32)
        nc.vector.memset(warm_in[:], 0.0)
        nc.scalar.activation(out=warm_out[:], in_=warm_in[:], func=ACT.Exp)

        ident = const.tile([P, P], F32)
        make_identity(nc, ident[:])

        w_sb = const.tile([P, 4, C], BF16)
        nc.sync.dma_start(out=w_sb[:], in_=w2.rearrange("(i j) c -> i j c", j=4))
        x_sb = []

        def load(b):
            row = []
            for k in range(3):
                xt = xin.tile([P, 4, C], BF16, name="x%d_%d" % (k, b), tag="x%d" % k)
                src = xs[k][b].rearrange("w h c -> (w h) c").rearrange("(p j) c -> p j c", j=4)
                nc.sync.dma_start(out=xt[:], in_=src)
                row.append(xt)
            x_sb.append(row)

        AHEAD = 6
        for b in range(AHEAD):
            load(b)

        aux_ps = psum.tile([P, 2, P], F32, tag="o")
        hat_w = hat_sb[:].bitcast(F32)
        for u in range(2):
            nc.tensor.transpose(aux_ps[:, u, :], hat_w[:, u : 2 * P : 2], ident[:])
        logit = const.tile([P, 16, 3, 2], F32)
        nc.vector.tensor_copy(
            out=logit[:].rearrange("q (u b) k e -> q u (b k e)", u=2),
            in_=aux_ps[:].bitcast(BF16)[:, :, 0:48],
        )
        top = const.tile([P, 16, 2], F32)
        nc.vector.tensor_reduce(
            out=top[:], in_=logit[:].rearrange("q a k e -> q a e k"), axis=AX.X, op=ALU.max
        )
        shifted = const.tile([P, 16, 3, 2], F32)
        nc.vector.tensor_tensor(
            out=shifted[:], in0=logit[:], in1=top[:].unsqueeze(2).to_broadcast([P, 16, 3, 2]),
            op=ALU.subtract,
        )
        expd = const.tile([P, 16, 3, 2], F32)
        nc.scalar.activation(out=expd[:], in_=shifted[:], func=ACT.Exp)
        total = const.tile([P, 16, 2], F32)
        nc.vector.tensor_reduce(
            out=total[:], in_=expd[:].rearrange("q a k e -> q a e k"), axis=AX.X, op=ALU.add
        )
        inv = const.tile([P, 16, 2], F32)
        nc.vector.reciprocal(out=inv[:], in_=total[:])
        gate = const.tile([P, 16, 3, 2], F32)
        nc.vector.tensor_tensor(
            out=gate[:], in0=expd[:], in1=inv[:].unsqueeze(2).to_broadcast([P, 16, 3, 2]),
            op=ALU.mult,
        )

        w_codes = const.tile([P, C], U32, align_bytes=64)
        w_scales = const.tile([P, C], U8, align_bytes=64)
        w_grouped = const.tile([P, 4 * C], BF16, align_bytes=64)
        w_words = w_sb[:].bitcast(F32)
        w_pairs = w_grouped[:].bitcast(F32).rearrange("q (c u) -> q c u", u=2)
        for h in range(2):
            w_ps = psum.tile([P, 2, 2, P], F32, tag="o")
            for u in range(2):
                for jj in range(2):
                    nc.tensor.transpose(
                        w_ps[:, u, jj, :], w_words[:, 2 * h + jj, u : 2 * P : 2], ident[:]
                    )
            copy = nc.vector.tensor_copy if h == 0 else nc.scalar.copy
            copy(
                out=w_pairs[:, 256 * h : 256 * h + 256, :],
                in_=w_ps[:].rearrange("q u jj i -> q (jj i) u"),
            )
        b2_f = const.tile([P, 4], F32)
        nc.vector.tensor_copy(out=b2_f[:], in_=b2_bf[:])
        nc.vector.quantize_mx(out=w_codes[:].bitcast(FP8X4), scales=w_scales[:], in_=w_grouped[:])

        def half_view(bank, e):
            v = bank[:].bitcast(BF16).rearrange("q j (p e) -> q j p e", e=2)
            return v[:, :, :, e].rearrange("q j p -> q p j")

        banks = {}
        t0s = {}
        t1s = {}
        planes = {}
        grouped = {}
        codes = {}
        scales = {}
        o_sbs = {}

        def gate_of(n, k, e):
            return gate[:, 8 * (n % 2) + n // 2, k, e : e + 1]

        def transposes(n, k):
            if n >= UNITS:
                return
            b, u = n // 2, n % 2
            bank = psum.tile([P, 4, P], F32, name="bank%d" % k, tag="t%d" % k)
            xw = x_sb[b][k][:].bitcast(F32)
            for j in range(4):
                nc.tensor.transpose(bank[:, j, :], xw[:, j, u : 2 * P : 2], ident[:])
            banks[(n, k)] = bank

        def pass1(n):
            if n >= UNITS:
                return
            for e in range(2):
                t0 = work.tile([P, P, 4], F32, name="t0", bufs=8)
                nc.scalar.activation(
                    out=t0[:], in_=half_view(banks[(n, 0)], e), func=ACT.Copy, scale=gate_of(n, 0, e)
                )
                t0s[(n, e)] = t0

        def pass2(n, e):
            t1 = work.tile([P, P, 4], F32, name="t1")
            nc.vector.scalar_tensor_tensor(
                out=t1[:], in0=half_view(banks[(n, 1)], e), scalar=gate_of(n, 1, e),
                in1=t0s[(n, e)][:], op0=ALU.mult, op1=ALU.add,
            )
            t1s[(n, e)] = t1

        def pass3(n):
            b, u = n // 2, n % 2
            if u == 0:
                planes[b] = stage.tile([P, 4, TOK], BF16, name="planes")
            for e in range(2):
                nc.vector.scalar_tensor_tensor(
                    out=planes[b][:, 2 * u + e, :].rearrange("q (p j) -> q p j", j=4),
                    in0=half_view(banks[(n, 2)], e), scalar=gate_of(n, 2, e),
                    in1=t1s[(n, e)][:], op0=ALU.mult, op1=ALU.add,
                )

        def regroup(b):
            grouped[b] = stage.tile([P, TOK, 4], BF16, name="grouped", align_bytes=64)
            nc.gpsimd.tensor_scalar(
                out=grouped[b][:], in0=planes[b][:].rearrange("q t n -> q n t"), scalar1=1.0,
                scalar2=0.0, op0=ALU.mult, op1=ALU.add,
            )

        def quantise(b, lo, hi):
            if lo == 0:
                codes[b] = stage.tile([P, TOK], U32, name="codes", align_bytes=64)
                scales[b] = stage.tile([P, TOK], U8, name="scales", align_bytes=64)
            nc.vector.quantize_mx(
                out=codes[b][:, lo:hi].bitcast(FP8X4), scales=scales[b][:, lo:hi],
                in_=grouped[b][:, lo:hi, :].rearrange("q n t -> q (n t)"),
            )

        def one_pass(b, j, lo, hi, tag):
            acc = psum.tile([P, hi - lo], F32, name="acc", tag=tag)
            nc.tensor.matmul_mx(
                out=acc[:],
                lhsT=w_codes[:, P * j : P * j + P].bitcast(FP8X4),
                lhsT_scale=w_scales[:, P * j : P * j + P],
                rhs=codes[b][:, lo:hi].bitcast(FP8X4),
                rhs_scale=scales[b][:, lo:hi],
                start=True,
                stop=True,
            )
            return acc

        def way_out(b, j, lo, hi, acc, on_vector):
            if on_vector:
                nc.vector.tensor_scalar_add(
                    out=o_sbs[b][:, j, lo:hi], in0=acc[:], scalar1=b2_f[:, j : j + 1]
                )
            else:
                nc.scalar.activation(
                    out=o_sbs[b][:, j, lo:hi], in_=acc[:], func=ACT.Identity,
                    bias=b2_f[:, j : j + 1], scale=1.0,
                )

        def store(b, j0, lo, hi, eng):
            dst = out[b].rearrange("(i j) w h -> i j (w h)", j=4)
            eng.dma_start(out=dst[:, j0 : j0 + 2, lo:hi], in_=o_sbs[b][:, j0 : j0 + 2, lo:hi])

        def project(b, j0, tag):
            if j0 == 0:
                o_sbs[b] = stage.tile([P, 4, TOK], F32, name="o_sb")
            for j in (j0, j0 + 1):
                way_out(b, j, 0, TOK, one_pass(b, j, 0, TOK, tag), False)
            store(b, j0, 0, TOK, nc.sync)
            if j0 == 2 and b + AHEAD < B:
                load(b + AHEAD)

        for n in range(2):
            for k in range(3):
                transposes(n, k)
            pass1(n)
        transposes(2, 0)
        pass1(2)
        for n in range(UNITS):
            transposes(n + 3, 0)
            pass1(n + 3)
            if n % 2 == 0 and n >= 4:
                project((n - 4) // 2, 2, "o")
            pass2(n, 0)
            if n == UNITS - 1:
                quantise(B - 2, 0, TOK)
                project(B - 2, 0, "o")
                project(B - 2, 2, "t0")
            pass2(n, 1)
            transposes(n + 2, 1)
            if n % 2 == 1 and 3 <= n < UNITS - 1:
                quantise((n - 3) // 2, 0, TOK)
                project((n - 3) // 2, 0, "o")
            pass3(n)
            transposes(n + 2, 2)
            if n % 2 == 1 and n < UNITS - 1:
                regroup(n // 2)

        b = B - 1
        HALF = TOK // 2
        g = stage.tile([P, TOK, 4], BF16, name="grouped", align_bytes=64)
        grouped[b] = g
        src = planes[b][:].rearrange("q t n -> q n t")
        nc.vector.tensor_copy(out=g[:, 0:HALF, :], in_=src[:, 0:HALF, :])
        nc.gpsimd.tensor_scalar(
            out=g[:, 384:TOK, :], in0=src[:, 384:TOK, :], scalar1=1.0, scalar2=0.0,
            op0=ALU.mult, op1=ALU.add,
        )
        nc.vector.tensor_copy(out=g[:, HALF:384, :], in_=src[:, HALF:384, :])
        quantise(b, 0, HALF)
        quantise(b, HALF, TOK)
        o_sbs[b] = stage.tile([P, 4, TOK], F32, name="o_sb")
        for h, tags in ((0, ("t1", "t1", "t2", "t2")), (1, ("o", "o", "t0", "t0"))):
            lo, hi = h * HALF, h * HALF + HALF
            accs = [one_pass(b, j, lo, hi, tags[j]) for j in range(4)]
            for j in range(4):
                way_out(b, j, lo, hi, accs[j], j % 2 == 1)
                if j % 2 == 1:
                    store(b, j - 1, lo, hi, nc.sync)
